import numpy as np
import ml_dtypes


def mxq(x, axis, fmt="e4m3"):
    dtype, down = {"e4m3": (ml_dtypes.float8_e4m3fn, 7), "e5m2": (ml_dtypes.float8_e5m2, 14)}[fmt]
    v = np.moveaxis(np.asarray(x, np.float32).astype(ml_dtypes.bfloat16).astype(np.float64), axis, -1)
    blocks = v.reshape(v.shape[:-1] + (-1, 32))
    amax = np.abs(blocks).max(-1, keepdims=True)
    byte = np.maximum(np.where(amax > 0, np.frexp(amax)[1] - 1 + 127, 0) - down, 1)
    scale = np.exp2(byte - 127.0)
    codes = (blocks / scale).astype(np.float32).astype(dtype).astype(np.float64)
    return np.moveaxis((codes * scale).reshape(v.shape), -1, axis)


WIDE = False


def mx_kscale(k):
    if not WIDE:
        return np.ones(k)
    levels = np.array([10, -10, 5, -5, 0])
    if k % 512:
        return np.exp2(np.random.permutation(np.resize(levels, k // 32))).repeat(32)
    a = np.empty((k // 512, 16))
    for p in range(k // 512):
        a[p, :8] = np.random.permutation(np.resize(levels, 8))
        for g in range(8):
            far = levels[np.abs(levels - a[p, g]) >= 10]
            a[p, g + 8] = far[np.random.randint(len(far))]
    return np.exp2(a.ravel()).repeat(32)


BF16 = ml_dtypes.bfloat16


def bf(x):
    return np.asarray(x, np.float32).astype(BF16)


def f64(x):
    return np.asarray(x).astype(np.float64)


B, T, C, NH, HS, NLQ, NLKV, DHR = 1, 512, 2048, 16, 128, 512, 512, 128
THETA = 10000.0


def rope(v, cos, sin):
    vr = v.reshape(v.shape[:-1] + (-1, 2))
    re, im = vr[..., 0], vr[..., 1]
    c = cos[None, :, None, :]
    s = sin[None, :, None, :]
    return np.stack([re * c - im * s, re * s + im * c], axis=-1).reshape(v.shape)


def setup_inputs():
    s, t = mx_kscale(C), mx_kscale(NLQ)
    ang = np.outer(np.arange(T), 1.0 / THETA ** (np.arange(0, DHR, 2) / DHR))
    return {"x": bf(np.random.standard_normal((B, T, C)) * s),
            "cos": bf(np.cos(ang)),
            "sin": bf(np.sin(ang)),
            "W_dq": bf(np.random.standard_normal((NLQ, C)) / np.sqrt(C) / s[None, :] * t[:, None]),
            "W_uq": bf((np.random.standard_normal((NLQ, C)) / np.sqrt(NLQ) / t[:, None]).reshape(C, NLQ)),
            "W_uk": bf(np.random.standard_normal((C, NLKV)) / np.sqrt(HS)),
            "W_qr": bf(np.random.standard_normal((NH * DHR, NLQ)) / np.sqrt(NLQ) / t[None, :])}


def reference(x, cos, sin, W_dq, W_uq, W_uk, W_qr):
    cq = mxq(mxq(f64(x), 2, "e4m3") @ mxq(f64(W_dq), 1, "e4m3").T, 2, "e4m3")
    k_eff = f64(W_uq).reshape(NLQ, NH, HS).transpose(1, 0, 2) @ f64(W_uk).reshape(NH, HS, NLKV)
    q_abs = cq[:, None] @ mxq(k_eff, 1, "e4m3")[None]
    c_qr = (cq @ mxq(f64(W_qr), 1, "e4m3").T).reshape(B, T, NH, DHR)
    return q_abs, rope(c_qr, f64(cos), f64(sin))

@@ -1,0 +1,281 @@
+from contextlib import ExitStack
+
+import concourse.mybir as mybir
+from concourse.masks import make_identity
+
+F32 = mybir.dt.float32
+BF16 = mybir.dt.bfloat16
+U32 = mybir.dt.uint32
+U8 = mybir.dt.uint8
+FP8X4 = mybir.dt.float8_e4m3fn_x4
+MULT = mybir.AluOpType.mult
+ADD = mybir.AluOpType.add
+
+P = 128
+PACK = 4
+T = 512
+C = 2048
+L = 512
+NH = 16
+HS = 128
+N = 512
+O = 2048
+C_PASSES = C // (P * PACK)
+T_TILES = T // P
+BANK = 512
+O_BLOCKS = O // BANK
+FIRST_HEADS = 4
+QA_BANKS = ("qa", 3)
+KE_BANKS = ("ke", 3)
+TP_BANKS = ("tp", 1)
+
+FLOPS = 2 * (T * C * L + NH * L * HS * N + NH * T * L * N + T * L * O)
+
+
+def tile_causalselfattention_pa_kernel(tc, x, cos, sin, W_dq, W_uq, W_uk, W_qr, out_0, out_1):
+    nc = tc.nc
+    with ExitStack() as ctx:
+        ctx.enter_context(tc.manual_schedule())
+        const = ctx.enter_context(tc.tile_pool(name="const", bufs=1))
+        raw = ctx.enter_context(tc.tile_pool(name="raw", bufs=1))
+        codes = ctx.enter_context(tc.tile_pool(name="codes", bufs=1))
+        stage = ctx.enter_context(tc.tile_pool(name="stage", bufs=3))
+        results = ctx.enter_context(tc.tile_pool(name="results", bufs=2))
+        psum = ctx.enter_context(tc.psum_pool(name="psum", bufs=1))
+
+        wdq_raw = raw.tile([P, PACK, C], BF16)
+        wdq_rows = W_dq.rearrange("(p j) c -> j p c", j=PACK)
+        for j in range(PACK):
+            nc.sync.dma_start(out=wdq_raw[:, j, :], in_=wdq_rows[j])
+        x_raw = raw.tile([P, T_TILES, C], BF16)
+        x_rows = x.flatten_outer_dims().rearrange("(p r) c -> r p c", r=T_TILES)
+        for r in range(T_TILES):
+            nc.sync.dma_start(out=x_raw[:, r, :], in_=x_rows[r])
+        wuq_raw = raw.tile([P, PACK, NH * HS], BF16)
+        wuq_rows = W_uq.rearrange("(l a) b -> l (a b)", a=4).rearrange("(p j) c -> p j c", j=PACK)
+        wuk_raw = raw.tile([P, NH, N], BF16)
+        wuk_rows = W_uk.rearrange("(h d) n -> d h n", d=HS)
+        wqr_raw = raw.tile([P, O // 256, 2 * L], BF16)
+        wqr_rows = W_qr.rearrange("(a p e) l -> p a (e l)", p=P, e=2)
+        cos_raw = const.tile([P, T_TILES, HS // 2], BF16)
+        sin_raw = const.tile([P, T_TILES, HS // 2], BF16)
+
+        def load_a(first_head, end_head):
+            a_cols = slice(HS * first_head, HS * end_head)
+            nc.sync.dma_start(out=wuq_raw[:, :, a_cols], in_=wuq_rows[:, :, a_cols])
+
+        def load_block(b):
+            nc.sync.dma_start(out=wuk_raw[:, 4 * b : 4 * b + 4, :], in_=wuk_rows[:, 4 * b : 4 * b + 4, :])
+            nc.sync.dma_start(out=wqr_raw[:, 2 * b : 2 * b + 2, :], in_=wqr_rows[:, 2 * b : 2 * b + 2, :])
+
+        load_a(0, FIRST_HEADS)
+        load_block(0)
+        nc.sync.dma_start(out=cos_raw[:], in_=cos.rearrange("(p r) i -> p r i", r=T_TILES))
+        nc.sync.dma_start(out=sin_raw[:], in_=sin.rearrange("(p r) i -> p r i", r=T_TILES))
+        load_a(FIRST_HEADS, NH)
+        for b in range(1, O_BLOCKS):
+            load_block(b)
+
+        ident_f32 = const.tile([P, P], F32)
+        make_identity(nc, ident_f32[:])
+        ident_bf16 = const.tile([P, P], BF16)
+        make_identity(nc, ident_bf16[:])
+
+        cos_pairs = const.tile([P, T_TILES, P, 2], F32)
+        sin_signed = const.tile([P, T_TILES, 2, P], F32)
+        for r in range(T_TILES):
+            nc.gpsimd.tensor_scalar(
+                out=cos_pairs[:, r].rearrange("p (a i) e -> p a i e", a=2),
+                in0=cos_raw[:, r, :].unsqueeze(1).unsqueeze(3).to_broadcast([P, 2, HS // 2, 2]),
+                scalar1=1.0, scalar2=0.0, op0=MULT, op1=ADD,
+            )
+            for e in range(2):
+                nc.gpsimd.tensor_scalar(
+                    out=sin_signed[:, r, e, :].rearrange("p (a i) -> p a i", a=2),
+                    in0=sin_raw[:, r, :].unsqueeze(1).to_broadcast([P, 2, HS // 2]),
+                    scalar1=(-1.0 if e == 0 else 1.0), scalar2=0.0, op0=MULT, op1=ADD,
+                )
+
+        def leave_psum(on_scalar, out, in_):
+            if on_scalar:
+                nc.scalar.copy(out=out, in_=in_)
+            else:
+                nc.vector.tensor_copy(out=out, in_=in_)
+
+        def transpose_words(grouped, rows_a, rows_b, banks):
+            bank = psum.tile([P, 2, 2, P], F32, tag=banks[0], bufs=banks[1], name="words")
+            for run, rows in enumerate((rows_a, rows_b)):
+                for half in range(2):
+                    nc.tensor.transpose(bank[:, run, half, :], rows.bitcast(F32)[:, half : 2 * P : 2], ident_f32[:])
+            nc.scalar.copy(
+                out=grouped.bitcast(F32).rearrange("p (a c) w -> p a c w", a=2),
+                in_=bank[:].rearrange("p a w c -> p a c w"),
+            )
+
+        def quantise(grouped, words, scales):
+            nc.vector.quantize_mx(out=words.bitcast(FP8X4), scales=scales, in_=grouped.rearrange("p c k -> p (c k)"))
+
+        def quantise_rows(rows, words, scales):
+            grouped = stage.tile([P, C_PASSES * P, PACK], BF16, align_bytes=64)
+            for pair in range(C_PASSES // 2):
+                transpose_words(
+                    grouped[:, 256 * pair : 256 * pair + 256, :],
+                    rows[:, 1024 * pair : 1024 * pair + 512], rows[:, 1024 * pair + 512 : 1024 * pair + 1024], QA_BANKS,
+                )
+            quantise(grouped[:], words, scales)
+
+        wdq_words = codes.tile([P, PACK, C_PASSES * P], U32, align_bytes=64)
+        wdq_scales = codes.tile([P, PACK, C_PASSES * P], U8, align_bytes=64)
+        x_words = codes.tile([P, T_TILES, C_PASSES * P], U32, align_bytes=64)
+        x_scales = codes.tile([P, T_TILES, C_PASSES * P], U8, align_bytes=64)
+        cq_words = codes.tile([P, T], U32, align_bytes=64)
+        cq_scales = codes.tile([P, T], U8, align_bytes=64)
+
+        def make_c_q(r):
+            cq_bank = psum.tile([P, PACK, P], F32, tag=KE_BANKS[0], bufs=KE_BANKS[1])
+            for j in range(PACK):
+                for g in range(C_PASSES):
+                    k_cols = slice(P * g, P * g + P)
+                    nc.tensor.matmul_mx(
+                        out=cq_bank[:, j, :],
+                        lhsT=wdq_words[:, j, k_cols].bitcast(FP8X4), lhsT_scale=wdq_scales[:, j, k_cols],
+                        rhs=x_words[:, r, k_cols].bitcast(FP8X4), rhs_scale=x_scales[:, r, k_cols],
+                        start=(g == 0), stop=(g == C_PASSES - 1),
+                    )
+            cq_grouped = stage.tile([P, P, PACK], BF16, align_bytes=64)
+            leave_psum(r % 2 == 1, out=cq_grouped[:], in_=cq_bank[:].rearrange("p j t -> p t j"))
+            quantise(cq_grouped[:], cq_words[:, P * r : P * r + P], cq_scales[:, P * r : P * r + P])
+
+        wqr_words = codes.tile([P, O], U32, align_bytes=64)
+        wqr_scales = codes.tile([P, O], U8, align_bytes=64)
+        wqr_grouped = {}
+
+        def transpose_wqr(b, a, banks):
+            if a == 0:
+                wqr_grouped[b] = stage.tile([P, BANK, PACK], BF16, align_bytes=64, name="wqr_grouped", bufs=2)
+            transpose_words(
+                wqr_grouped[b][:, 256 * a : 256 * a + 256, :],
+                wqr_raw[:, 2 * b + a, 0:L], wqr_raw[:, 2 * b + a, L : 2 * L], banks,
+            )
+
+        def quantise_wqr(b):
+            cols = slice(BANK * b, BANK * b + BANK)
+            quantise(wqr_grouped[b][:], wqr_words[:, cols], wqr_scales[:, cols])
+
+        a_t = {}
+
+        def transpose_a(h, banks):
+            at_bank = psum.tile([P, PACK, P], BF16, tag=banks[0], bufs=banks[1])
+            for j in range(PACK):
+                nc.tensor.transpose(at_bank[:, j, :], wuq_raw[:, j, HS * h : HS * h + HS], ident_bf16[:])
+            a_t[h] = stage.tile([P, PACK, P], BF16, name="a_t", bufs=5)
+            nc.scalar.copy(out=a_t[h][:], in_=at_bank[:])
+
+        ke_grouped = {}
+        ke_words = {}
+        ke_scales = {}
+
+        def make_k_eff(h, i, on_scalar):
+            if i == 0:
+                ke_grouped[h] = stage.tile([P, N, PACK], BF16, align_bytes=64, name="ke_grouped")
+            ke_bank = psum.tile([P, PACK, P], F32, tag=KE_BANKS[0], bufs=KE_BANKS[1])
+            for j in range(PACK):
+                nc.tensor.matmul(ke_bank[:, j, :], lhsT=a_t[h][:, j, :], rhs=wuk_raw[:, h, P * i : P * i + P], start=True, stop=True)
+            leave_psum(on_scalar, out=ke_grouped[h][:, P * i : P * i + P, :], in_=ke_bank[:].rearrange("p j n -> p n j"))
+
+        def quantise_k_eff(h):
+            ke_words[h] = stage.tile([P, N], U32, align_bytes=64, name="ke_words")
+            ke_scales[h] = stage.tile([P, N], U8, align_bytes=64, name="ke_scales")
+            quantise(ke_grouped[h][:], ke_words[h][:], ke_scales[h][:])
+
+        q_abs_rows = out_0.flatten_outer_dims().rearrange("(h p r) n -> h p r n", h=NH, r=T_TILES)
+        q_abs = {}
+
+        def make_q_abs(h, r):
+            if r == 0:
+                q_abs[h] = results.tile([P, T_TILES, N], F32, name="q_abs", bufs=3)
+            qa_bank = psum.tile([P, N], F32, tag=QA_BANKS[0], bufs=QA_BANKS[1])
+            nc.tensor.matmul_mx(
+                out=qa_bank[:],
+                lhsT=cq_words[:, P * r : P * r + P].bitcast(FP8X4), lhsT_scale=cq_scales[:, P * r : P * r + P],
+                rhs=ke_words[h][:].bitcast(FP8X4), rhs_scale=ke_scales[h][:],
+                start=True, stop=True,
+            )
+            nc.scalar.copy(out=q_abs[h][:, r, :], in_=qa_bank[:])
+            if r == T_TILES - 1:
+                nc.sync.dma_start(out=q_abs_rows[h], in_=q_abs[h][:])
+
+        q_r_rows = out_1.rearrange("b t h d -> (b t) (h d)").rearrange("(p r) o -> p r o", r=T_TILES)
+        c_qr = {}
+
+        def make_c_qr(bank_no):
+            b, r = divmod(bank_no, T_TILES)
+            cols = slice(BANK * b, BANK * b + BANK)
+            c_qr[bank_no] = psum.tile([P, 2, 2, P], F32, tag="cr", bufs=1, name="cr_bank")
+            nc.tensor.matmul_mx(
+                out=c_qr[bank_no][:].rearrange("p a e c -> p (a e c)"),
+                lhsT=cq_words[:, P * r : P * r + P].bitcast(FP8X4), lhsT_scale=cq_scales[:, P * r : P * r + P],
+                rhs=wqr_words[:, cols].bitcast(FP8X4), rhs_scale=wqr_scales[:, cols],
+                start=True, stop=True,
+            )
+
+        def rotate(bank_no):
+            b, r = divmod(bank_no, T_TILES)
+            cr_bank = c_qr[bank_no]
+            q_r = results.tile([P, BANK], F32, bufs=3)
+            same = results.tile([P, 2, P, 2], F32)
+            nc.vector.tensor_tensor(
+                out=same[:], in0=cr_bank[:].rearrange("p a e c -> p a c e"),
+                in1=cos_pairs[:, r].unsqueeze(1).to_broadcast([P, 2, P, 2]), op=MULT,
+            )
+            cross = results.tile([P, 2, 2, P], F32)
+            for e in range(2):
+                nc.vector.tensor_tensor(
+                    out=cross[:, e], in0=cr_bank[:, :, 1 - e, :],
+                    in1=sin_signed[:, r, e, :].unsqueeze(1).to_broadcast([P, 2, P]), op=MULT,
+                )
+            nc.gpsimd.tensor_tensor(
+                out=q_r[:].rearrange("p (a c e) -> p a c e", a=2, e=2),
+                in0=same[:], in1=cross[:].rearrange("p e a c -> p a c e"), op=ADD,
+            )
+            nc.sync.dma_start(out=q_r_rows[:, r, BANK * b : BANK * b + BANK], in_=q_r[:])
+
+        for j in range(PACK):
+            quantise_rows(wdq_raw[:, j, :], wdq_words[:, j, :], wdq_scales[:, j, :])
+        for r in range(T_TILES + 2):
+            if r < T_TILES:
+                quantise_rows(x_raw[:, r, :], x_words[:, r, :], x_scales[:, r, :])
+            if r == T_TILES - 1:
+                transpose_a(0, QA_BANKS)
+            if r >= 2:
+                make_c_q(r - 2)
+        for i in range(4):
+            make_k_eff(0, i, False)
+            if i < 2:
+                transpose_wqr(0, i, QA_BANKS)
+            else:
+                transpose_a(i - 1, QA_BANKS)
+        transpose_a(3, QA_BANKS)
+        quantise_wqr(0)
+        quantise_k_eff(0)
+        for i in range(4):
+            make_k_eff(1, i, True)
+        make_c_qr(0)
+
+        for h in range(NH):
+            next_block = h // T_TILES + 1
+            if h + 4 < NH:
+                transpose_a(h + 4, TP_BANKS)
+            rotate(h)
+            if h + 1 < NH:
+                quantise_k_eff(h + 1)
+            if h % T_TILES == 2 and next_block < O_BLOCKS:
+                quantise_wqr(next_block)
+            for i in range(4):
+                make_q_abs(h, i)
+                if i == 3 and h + 1 < NH:
+                    make_c_qr(h + 1)
+                if h + 2 < NH:
+                    make_k_eff(h + 2, i, i == 3 or (i == 0 and h % T_TILES == 2))
+                if i == 1 and h % T_TILES < 2 and next_block < O_BLOCKS:
+                    transpose_wqr(next_block, h % T_TILES, TP_BANKS)

@@ -25,9 +25,7 @@ T_TILES = T // P
 BANK = 512
 O_BLOCKS = O // BANK
 FIRST_HEADS = 4
-QA_BANKS = ("qa", 3)
-KE_BANKS = ("ke", 3)
-TP_BANKS = ("tp", 1)
+BANKS = ("ps", 8)
 
 FLOPS = 2 * (T * C * L + NH * L * HS * N + NH * T * L * N + T * L * O)
 
@@ -120,7 +118,7 @@ def tile_causalselfattention_pa_kernel(tc, x, cos, sin, W_dq, W_uq, W_uk, W_qr, 
             for pair in range(C_PASSES // 2):
                 transpose_words(
                     grouped[:, 256 * pair : 256 * pair + 256, :],
-                    rows[:, 1024 * pair : 1024 * pair + 512], rows[:, 1024 * pair + 512 : 1024 * pair + 1024], QA_BANKS,
+                    rows[:, 1024 * pair : 1024 * pair + 512], rows[:, 1024 * pair + 512 : 1024 * pair + 1024], BANKS,
                 )
             quantise(grouped[:], words, scales)
 
@@ -132,7 +130,7 @@ def tile_causalselfattention_pa_kernel(tc, x, cos, sin, W_dq, W_uq, W_uk, W_qr, 
         cq_scales = codes.tile([P, T], U8, align_bytes=64)
 
         def make_c_q(r):
-            cq_bank = psum.tile([P, PACK, P], F32, tag=KE_BANKS[0], bufs=KE_BANKS[1])
+            cq_bank = psum.tile([P, PACK, P], F32, tag=BANKS[0], bufs=BANKS[1])
             for j in range(PACK):
                 for g in range(C_PASSES):
                     k_cols = slice(P * g, P * g + P)
@@ -165,11 +163,13 @@ def tile_causalselfattention_pa_kernel(tc, x, cos, sin, W_dq, W_uq, W_uk, W_qr, 
         a_t = {}
 
         def transpose_a(h, banks):
-            at_bank = psum.tile([P, PACK, P], BF16, tag=banks[0], bufs=banks[1])
-            for j in range(PACK):
-                nc.tensor.transpose(at_bank[:, j, :], wuq_raw[:, j, HS * h : HS * h + HS], ident_bf16[:])
-            a_t[h] = stage.tile([P, PACK, P], BF16, name="a_t", bufs=5)
-            nc.scalar.copy(out=a_t[h][:], in_=at_bank[:])
+            at_bank = psum.tile([P, 2, PACK, P], BF16, tag=banks[0], bufs=banks[1])
+            for n in range(2):
+                for j in range(PACK):
+                    nc.tensor.transpose(at_bank[:, n, j, :], wuq_raw[:, j, HS * (h + n) : HS * (h + n) + HS], ident_bf16[:])
+            pair = stage.tile([P, 2, PACK, P], BF16, name="a_t", bufs=3)
+            nc.scalar.copy(out=pair[:], in_=at_bank[:])
+            a_t[h], a_t[h + 1] = pair[:, 0], pair[:, 1]
 
         ke_grouped = {}
         ke_words = {}
@@ -178,7 +178,7 @@ def tile_causalselfattention_pa_kernel(tc, x, cos, sin, W_dq, W_uq, W_uk, W_qr, 
         def make_k_eff(h, i, on_scalar):
             if i == 0:
                 ke_grouped[h] = stage.tile([P, N, PACK], BF16, align_bytes=64, name="ke_grouped")
-            ke_bank = psum.tile([P, PACK, P], F32, tag=KE_BANKS[0], bufs=KE_BANKS[1])
+            ke_bank = psum.tile([P, PACK, P], F32, tag=BANKS[0], bufs=BANKS[1])
             for j in range(PACK):
                 nc.tensor.matmul(ke_bank[:, j, :], lhsT=a_t[h][:, j, :], rhs=wuk_raw[:, h, P * i : P * i + P], start=True, stop=True)
             leave_psum(on_scalar, out=ke_grouped[h][:, P * i : P * i + P, :], in_=ke_bank[:].rearrange("p j n -> p n j"))
@@ -194,7 +194,7 @@ def tile_causalselfattention_pa_kernel(tc, x, cos, sin, W_dq, W_uq, W_uk, W_qr, 
         def make_q_abs(h, r):
             if r == 0:
                 q_abs[h] = results.tile([P, T_TILES, N], F32, name="q_abs", bufs=3)
-            qa_bank = psum.tile([P, N], F32, tag=QA_BANKS[0], bufs=QA_BANKS[1])
+            qa_bank = psum.tile([P, N], F32, tag=BANKS[0], bufs=BANKS[1])
             nc.tensor.matmul_mx(
                 out=qa_bank[:],
                 lhsT=cq_words[:, P * r : P * r + P].bitcast(FP8X4), lhsT_scale=cq_scales[:, P * r : P * r + P],
@@ -211,7 +211,7 @@ def tile_causalselfattention_pa_kernel(tc, x, cos, sin, W_dq, W_uq, W_uk, W_qr, 
         def make_c_qr(bank_no):
             b, r = divmod(bank_no, T_TILES)
             cols = slice(BANK * b, BANK * b + BANK)
-            c_qr[bank_no] = psum.tile([P, 2, 2, P], F32, tag="cr", bufs=1, name="cr_bank")
+            c_qr[bank_no] = psum.tile([P, 2, 2, P], F32, tag=BANKS[0], bufs=BANKS[1], name="cr_bank")
             nc.tensor.matmul_mx(
                 out=c_qr[bank_no][:].rearrange("p a e c -> p (a e c)"),
                 lhsT=cq_words[:, P * r : P * r + P].bitcast(FP8X4), lhsT_scale=cq_scales[:, P * r : P * r + P],
@@ -246,16 +246,15 @@ def tile_causalselfattention_pa_kernel(tc, x, cos, sin, W_dq, W_uq, W_uk, W_qr, 
             if r < T_TILES:
                 quantise_rows(x_raw[:, r, :], x_words[:, r, :], x_scales[:, r, :])
             if r == T_TILES - 1:
-                transpose_a(0, QA_BANKS)
+                transpose_a(0, BANKS)
             if r >= 2:
                 make_c_q(r - 2)
         for i in range(4):
             make_k_eff(0, i, False)
             if i < 2:
-                transpose_wqr(0, i, QA_BANKS)
-            else:
-                transpose_a(i - 1, QA_BANKS)
-        transpose_a(3, QA_BANKS)
+                transpose_wqr(0, i, BANKS)
+            elif i == 2:
+                transpose_a(2, BANKS)
         quantise_wqr(0)
         quantise_k_eff(0)
         for i in range(4):
@@ -264,18 +263,20 @@ def tile_causalselfattention_pa_kernel(tc, x, cos, sin, W_dq, W_uq, W_uk, W_qr, 
 
         for h in range(NH):
             next_block = h // T_TILES + 1
-            if h + 4 < NH:
-                transpose_a(h + 4, TP_BANKS)
+            if h % 2 == 0 and h + 4 < NH:
+                transpose_a(h + 4, BANKS)
+            if h % T_TILES == 0 and next_block < O_BLOCKS:
+                transpose_wqr(next_block, 0, BANKS)
+            if h % T_TILES == 2 and next_block < O_BLOCKS:
+                transpose_wqr(next_block, 1, BANKS)
             rotate(h)
             if h + 1 < NH:
                 quantise_k_eff(h + 1)
-            if h % T_TILES == 2 and next_block < O_BLOCKS:
+            if h % T_TILES == 3 and next_block < O_BLOCKS:
                 quantise_wqr(next_block)
             for i in range(4):
                 make_q_abs(h, i)
                 if i == 3 and h + 1 < NH:
                     make_c_qr(h + 1)
                 if h + 2 < NH:
-                    make_k_eff(h + 2, i, i == 3 or (i == 0 and h % T_TILES == 2))
-                if i == 1 and h % T_TILES < 2 and next_block < O_BLOCKS:
-                    transpose_wqr(next_block, h % T_TILES, TP_BANKS)
+                    make_k_eff(h + 2, i, i == 3 or (i == 0 and h % T_TILES == 3))

@@ -191,7 +191,7 @@ def tile_causalselfattention_pa_kernel(tc, x, cos, sin, W_dq, W_uq, W_uk, W_qr, 
         q_abs_rows = out_0.flatten_outer_dims().rearrange("(h p r) n -> h p r n", h=NH, r=T_TILES)
         q_abs = {}
 
-        def make_q_abs(h, r):
+        def make_q_abs(h, r, on_scalar):
             if r == 0:
                 q_abs[h] = results.tile([P, T_TILES, N], F32, name="q_abs", bufs=3)
             qa_bank = psum.tile([P, N], F32, tag=BANKS[0], bufs=BANKS[1])
@@ -201,12 +201,13 @@ def tile_causalselfattention_pa_kernel(tc, x, cos, sin, W_dq, W_uq, W_uk, W_qr, 
                 rhs=ke_words[h][:].bitcast(FP8X4), rhs_scale=ke_scales[h][:],
                 start=True, stop=True,
             )
-            nc.scalar.copy(out=q_abs[h][:, r, :], in_=qa_bank[:])
-            if r == T_TILES - 1:
-                nc.sync.dma_start(out=q_abs_rows[h], in_=q_abs[h][:])
+            leave_psum(on_scalar, out=q_abs[h][:, r, :], in_=qa_bank[:])
+            if r % 2 == 1:
+                nc.sync.dma_start(out=q_abs_rows[h, :, r - 1 : r + 1, :], in_=q_abs[h][:, r - 1 : r + 1, :])
 
         q_r_rows = out_1.rearrange("b t h d -> (b t) (h d)").rearrange("(p r) o -> p r o", r=T_TILES)
         c_qr = {}
+        q_r = {}
 
         def make_c_qr(bank_no):
             b, r = divmod(bank_no, T_TILES)
@@ -220,9 +221,9 @@ def tile_causalselfattention_pa_kernel(tc, x, cos, sin, W_dq, W_uq, W_uk, W_qr, 
             )
 
         def rotate(bank_no):
-            b, r = divmod(bank_no, T_TILES)
+            r = bank_no % T_TILES
             cr_bank = c_qr[bank_no]
-            q_r = results.tile([P, BANK], F32, bufs=3)
+            q_r[bank_no] = results.tile([P, BANK], F32, name="q_r", bufs=3)
             same = results.tile([P, 2, P, 2], F32)
             nc.vector.tensor_tensor(
                 out=same[:], in0=cr_bank[:].rearrange("p a e c -> p a c e"),
@@ -235,10 +236,13 @@ def tile_causalselfattention_pa_kernel(tc, x, cos, sin, W_dq, W_uq, W_uk, W_qr, 
                     in1=sin_signed[:, r, e, :].unsqueeze(1).to_broadcast([P, 2, P]), op=MULT,
                 )
             nc.gpsimd.tensor_tensor(
-                out=q_r[:].rearrange("p (a c e) -> p a c e", a=2, e=2),
+                out=q_r[bank_no][:].rearrange("p (a c e) -> p a c e", a=2, e=2),
                 in0=same[:], in1=cross[:].rearrange("p e a c -> p a c e"), op=ADD,
             )
-            nc.sync.dma_start(out=q_r_rows[:, r, BANK * b : BANK * b + BANK], in_=q_r[:])
+
+        def store_q_r(bank_no):
+            b, r = divmod(bank_no, T_TILES)
+            nc.sync.dma_start(out=q_r_rows[:, r, BANK * b : BANK * b + BANK], in_=q_r[bank_no][:])
 
         for j in range(PACK):
             quantise_rows(wdq_raw[:, j, :], wdq_words[:, j, :], wdq_scales[:, j, :])
@@ -275,8 +279,9 @@ def tile_causalselfattention_pa_kernel(tc, x, cos, sin, W_dq, W_uq, W_uk, W_qr, 
             if h % T_TILES == 3 and next_block < O_BLOCKS:
                 quantise_wqr(next_block)
             for i in range(4):
-                make_q_abs(h, i)
+                make_q_abs(h, i, h < NH - 1 or i % 2 == 1)
                 if i == 3 and h + 1 < NH:
                     make_c_qr(h + 1)
                 if h + 2 < NH:
                     make_k_eff(h + 2, i, i == 3 or (i == 0 and h % T_TILES == 3))
+            store_q_r(h)

@@ -43,7 +43,10 @@ def tile_causalselfattention_pa_kernel(tc, x, cos, sin, W_dq, W_uq, W_uk, W_qr, 
 
         wdq_raw = raw.tile([P, PACK, C], BF16)
         wdq_rows = W_dq.rearrange("(p j) c -> j p c", j=PACK)
-        for j in range(PACK):
+        for half in range(2):
+            c_half = slice(half * C // 2, (half + 1) * C // 2)
+            nc.sync.dma_start(out=wdq_raw[:, 0, c_half], in_=wdq_rows[0][:, c_half])
+        for j in range(1, PACK):
             nc.sync.dma_start(out=wdq_raw[:, j, :], in_=wdq_rows[j])
         x_raw = raw.tile([P, T_TILES, C], BF16)
         x_rows = x.flatten_outer_dims().rearrange("(p r) c -> r p c", r=T_TILES)
@@ -230,14 +233,13 @@ def tile_causalselfattention_pa_kernel(tc, x, cos, sin, W_dq, W_uq, W_uk, W_qr, 
                 in1=cos_pairs[:, r].unsqueeze(1).to_broadcast([P, 2, P, 2]), op=MULT,
             )
             cross = results.tile([P, 2, 2, P], F32)
-            for e in range(2):
-                nc.vector.tensor_tensor(
-                    out=cross[:, e], in0=cr_bank[:, :, 1 - e, :],
-                    in1=sin_signed[:, r, e, :].unsqueeze(1).to_broadcast([P, 2, P]), op=MULT,
-                )
+            nc.vector.tensor_tensor(
+                out=cross[:], in0=cr_bank[:, :, ::-1, :],
+                in1=sin_signed[:, r].unsqueeze(1).to_broadcast([P, 2, 2, P]), op=MULT,
+            )
             nc.gpsimd.tensor_tensor(
                 out=q_r[bank_no][:].rearrange("p (a c e) -> p a c e", a=2, e=2),
-                in0=same[:], in1=cross[:].rearrange("p e a c -> p a c e"), op=ADD,
+                in0=same[:], in1=cross[:].rearrange("p a e c -> p a c e"), op=ADD,
             )
 
         def store_q_r(bank_no):

@@ -269,8 +269,8 @@ def tile_causalselfattention_pa_kernel(tc, x, cos, sin, W_dq, W_uq, W_uk, W_qr, 
 
         for h in range(NH):
             next_block = h // T_TILES + 1
-            if h % 2 == 0 and h + 4 < NH:
-                transpose_a(h + 4, BANKS)
+            if h % 2 == 1 and h + 3 < NH:
+                transpose_a(h + 3, BANKS)
             if h % T_TILES == 0 and next_block < O_BLOCKS:
                 transpose_wqr(next_block, 0, BANKS)
             if h % T_TILES == 2 and next_block < O_BLOCKS:

from contextlib import ExitStack

import concourse.mybir as mybir
from concourse.masks import make_identity

F32 = mybir.dt.float32
BF16 = mybir.dt.bfloat16
U32 = mybir.dt.uint32
U8 = mybir.dt.uint8
FP8X4 = mybir.dt.float8_e4m3fn_x4
MULT = mybir.AluOpType.mult
ADD = mybir.AluOpType.add

P = 128
PACK = 4
T = 512
C = 2048
L = 512
NH = 16
HS = 128
N = 512
O = 2048
C_PASSES = C // (P * PACK)
T_TILES = T // P
BANK = 512
O_BLOCKS = O // BANK
FIRST_HEADS = 4
BANKS = ("ps", 8)

FLOPS = 2 * (T * C * L + NH * L * HS * N + NH * T * L * N + T * L * O)


def tile_causalselfattention_pa_kernel(tc, x, cos, sin, W_dq, W_uq, W_uk, W_qr, out_0, out_1):
    nc = tc.nc
    with ExitStack() as ctx:
        ctx.enter_context(tc.manual_schedule())
        const = ctx.enter_context(tc.tile_pool(name="const", bufs=1))
        raw = ctx.enter_context(tc.tile_pool(name="raw", bufs=1))
        codes = ctx.enter_context(tc.tile_pool(name="codes", bufs=1))
        stage = ctx.enter_context(tc.tile_pool(name="stage", bufs=3))
        results = ctx.enter_context(tc.tile_pool(name="results", bufs=2))
        psum = ctx.enter_context(tc.psum_pool(name="psum", bufs=1))

        wdq_raw = raw.tile([P, PACK, C], BF16)
        wdq_rows = W_dq.rearrange("(p j) c -> j p c", j=PACK)
        for half in range(2):
            c_half = slice(half * C // 2, (half + 1) * C // 2)
            nc.sync.dma_start(out=wdq_raw[:, 0, c_half], in_=wdq_rows[0][:, c_half])
        for j in range(1, PACK):
            nc.sync.dma_start(out=wdq_raw[:, j, :], in_=wdq_rows[j])
        x_raw = raw.tile([P, T_TILES, C], BF16)
        x_rows = x.flatten_outer_dims().rearrange("(p r) c -> r p c", r=T_TILES)
        for r in range(T_TILES):
            nc.sync.dma_start(out=x_raw[:, r, :], in_=x_rows[r])
        wuq_raw = raw.tile([P, PACK, NH * HS], BF16)
        wuq_rows = W_uq.rearrange("(l a) b -> l (a b)", a=4).rearrange("(p j) c -> p j c", j=PACK)
        wuk_raw = raw.tile([P, NH, N], BF16)
        wuk_rows = W_uk.rearrange("(h d) n -> d h n", d=HS)
        wqr_raw = raw.tile([P, O // 256, 2 * L], BF16)
        wqr_rows = W_qr.rearrange("(a p e) l -> p a (e l)", p=P, e=2)
        cos_raw = const.tile([P, T_TILES, HS // 2], BF16)
        sin_raw = const.tile([P, T_TILES, HS // 2], BF16)

        def load_a(first_head, end_head):
            a_cols = slice(HS * first_head, HS * end_head)
            nc.sync.dma_start(out=wuq_raw[:, :, a_cols], in_=wuq_rows[:, :, a_cols])

        def load_block(b):
            nc.sync.dma_start(out=wuk_raw[:, 4 * b : 4 * b + 4, :], in_=wuk_rows[:, 4 * b : 4 * b + 4, :])
            nc.sync.dma_start(out=wqr_raw[:, 2 * b : 2 * b + 2, :], in_=wqr_rows[:, 2 * b : 2 * b + 2, :])

        load_a(0, FIRST_HEADS)
        load_block(0)
        nc.sync.dma_start(out=cos_raw[:], in_=cos.rearrange("(p r) i -> p r i", r=T_TILES))
        nc.sync.dma_start(out=sin_raw[:], in_=sin.rearrange("(p r) i -> p r i", r=T_TILES))
        load_a(FIRST_HEADS, NH)
        for b in range(1, O_BLOCKS):
            load_block(b)

        ident_f32 = const.tile([P, P], F32)
        make_identity(nc, ident_f32[:])
        ident_bf16 = const.tile([P, P], BF16)
        make_identity(nc, ident_bf16[:])

        cos_pairs = const.tile([P, T_TILES, P, 2], F32)
        sin_signed = const.tile([P, T_TILES, 2, P], F32)
        for r in range(T_TILES):
            nc.gpsimd.tensor_scalar(
                out=cos_pairs[:, r].rearrange("p (a i) e -> p a i e", a=2),
                in0=cos_raw[:, r, :].unsqueeze(1).unsqueeze(3).to_broadcast([P, 2, HS // 2, 2]),
                scalar1=1.0, scalar2=0.0, op0=MULT, op1=ADD,
            )
            for e in range(2):
                nc.gpsimd.tensor_scalar(
                    out=sin_signed[:, r, e, :].rearrange("p (a i) -> p a i", a=2),
                    in0=sin_raw[:, r, :].unsqueeze(1).to_broadcast([P, 2, HS // 2]),
                    scalar1=(-1.0 if e == 0 else 1.0), scalar2=0.0, op0=MULT, op1=ADD,
                )

        def leave_psum(on_scalar, out, in_):
            if on_scalar:
                nc.scalar.copy(out=out, in_=in_)
            else:
                nc.vector.tensor_copy(out=out, in_=in_)

        def transpose_words(grouped, rows_a, rows_b, banks):
            bank = psum.tile([P, 2, 2, P], F32, tag=banks[0], bufs=banks[1], name="words")
            for run, rows in enumerate((rows_a, rows_b)):
                for half in range(2):
                    nc.tensor.transpose(bank[:, run, half, :], rows.bitcast(F32)[:, half : 2 * P : 2], ident_f32[:])
            nc.scalar.copy(
                out=grouped.bitcast(F32).rearrange("p (a c) w -> p a c w", a=2),
                in_=bank[:].rearrange("p a w c -> p a c w"),
            )

        def quantise(grouped, words, scales):
            nc.vector.quantize_mx(out=words.bitcast(FP8X4), scales=scales, in_=grouped.rearrange("p c k -> p (c k)"))

        def quantise_rows(rows, words, scales):
            grouped = stage.tile([P, C_PASSES * P, PACK], BF16, align_bytes=64)
            for pair in range(C_PASSES // 2):
                transpose_words(
                    grouped[:, 256 * pair : 256 * pair + 256, :],
                    rows[:, 1024 * pair : 1024 * pair + 512], rows[:, 1024 * pair + 512 : 1024 * pair + 1024], BANKS,
                )
            quantise(grouped[:], words, scales)

        wdq_words = codes.tile([P, PACK, C_PASSES * P], U32, align_bytes=64)
        wdq_scales = codes.tile([P, PACK, C_PASSES * P], U8, align_bytes=64)
        x_words = codes.tile([P, T_TILES, C_PASSES * P], U32, align_bytes=64)
        x_scales = codes.tile([P, T_TILES, C_PASSES * P], U8, align_bytes=64)
        cq_words = codes.tile([P, T], U32, align_bytes=64)
        cq_scales = codes.tile([P, T], U8, align_bytes=64)

        def make_c_q(r):
            cq_bank = psum.tile([P, PACK, P], F32, tag=BANKS[0], bufs=BANKS[1])
            for j in range(PACK):
                for g in range(C_PASSES):
                    k_cols = slice(P * g, P * g + P)
                    nc.tensor.matmul_mx(
                        out=cq_bank[:, j, :],
                        lhsT=wdq_words[:, j, k_cols].bitcast(FP8X4), lhsT_scale=wdq_scales[:, j, k_cols],
                        rhs=x_words[:, r, k_cols].bitcast(FP8X4), rhs_scale=x_scales[:, r, k_cols],
                        start=(g == 0), stop=(g == C_PASSES - 1),
                    )
            cq_grouped = stage.tile([P, P, PACK], BF16, align_bytes=64)
            leave_psum(r % 2 == 1, out=cq_grouped[:], in_=cq_bank[:].rearrange("p j t -> p t j"))
            quantise(cq_grouped[:], cq_words[:, P * r : P * r + P], cq_scales[:, P * r : P * r + P])

        wqr_words = codes.tile([P, O], U32, align_bytes=64)
        wqr_scales = codes.tile([P, O], U8, align_bytes=64)
        wqr_grouped = {}

        def transpose_wqr(b, a, banks):
            if a == 0:
                wqr_grouped[b] = stage.tile([P, BANK, PACK], BF16, align_bytes=64, name="wqr_grouped", bufs=2)
            transpose_words(
                wqr_grouped[b][:, 256 * a : 256 * a + 256, :],
                wqr_raw[:, 2 * b + a, 0:L], wqr_raw[:, 2 * b + a, L : 2 * L], banks,
            )

        def quantise_wqr(b):
            cols = slice(BANK * b, BANK * b + BANK)
            quantise(wqr_grouped[b][:], wqr_words[:, cols], wqr_scales[:, cols])

        a_t = {}

        def transpose_a(h, banks):
            at_bank = psum.tile([P, 2, PACK, P], BF16, tag=banks[0], bufs=banks[1])
            for n in range(2):
                for j in range(PACK):
                    nc.tensor.transpose(at_bank[:, n, j, :], wuq_raw[:, j, HS * (h + n) : HS * (h + n) + HS], ident_bf16[:])
            pair = stage.tile([P, 2, PACK, P], BF16, name="a_t", bufs=3)
            nc.scalar.copy(out=pair[:], in_=at_bank[:])
            a_t[h], a_t[h + 1] = pair[:, 0], pair[:, 1]

        ke_grouped = {}
        ke_words = {}
        ke_scales = {}

        def make_k_eff(h, i, on_scalar):
            if i == 0:
                ke_grouped[h] = stage.tile([P, N, PACK], BF16, align_bytes=64, name="ke_grouped")
            ke_bank = psum.tile([P, PACK, P], F32, tag=BANKS[0], bufs=BANKS[1])
            for j in range(PACK):
                nc.tensor.matmul(ke_bank[:, j, :], lhsT=a_t[h][:, j, :], rhs=wuk_raw[:, h, P * i : P * i + P], start=True, stop=True)
            leave_psum(on_scalar, out=ke_grouped[h][:, P * i : P * i + P, :], in_=ke_bank[:].rearrange("p j n -> p n j"))

        def quantise_k_eff(h):
            ke_words[h] = stage.tile([P, N], U32, align_bytes=64, name="ke_words")
            ke_scales[h] = stage.tile([P, N], U8, align_bytes=64, name="ke_scales")
            quantise(ke_grouped[h][:], ke_words[h][:], ke_scales[h][:])

        q_abs_rows = out_0.flatten_outer_dims().rearrange("(h p r) n -> h p r n", h=NH, r=T_TILES)
        q_abs = {}

        def make_q_abs(h, r, on_scalar):
            if r == 0:
                q_abs[h] = results.tile([P, T_TILES, N], F32, name="q_abs", bufs=3)
            qa_bank = psum.tile([P, N], F32, tag=BANKS[0], bufs=BANKS[1])
            nc.tensor.matmul_mx(
                out=qa_bank[:],
                lhsT=cq_words[:, P * r : P * r + P].bitcast(FP8X4), lhsT_scale=cq_scales[:, P * r : P * r + P],
                rhs=ke_words[h][:].bitcast(FP8X4), rhs_scale=ke_scales[h][:],
                start=True, stop=True,
            )
            leave_psum(on_scalar, out=q_abs[h][:, r, :], in_=qa_bank[:])
            if r % 2 == 1:
                nc.sync.dma_start(out=q_abs_rows[h, :, r - 1 : r + 1, :], in_=q_abs[h][:, r - 1 : r + 1, :])

        q_r_rows = out_1.rearrange("b t h d -> (b t) (h d)").rearrange("(p r) o -> p r o", r=T_TILES)
        c_qr = {}
        q_r = {}

        def make_c_qr(bank_no):
            b, r = divmod(bank_no, T_TILES)
            cols = slice(BANK * b, BANK * b + BANK)
            c_qr[bank_no] = psum.tile([P, 2, 2, P], F32, tag=BANKS[0], bufs=BANKS[1], name="cr_bank")
            nc.tensor.matmul_mx(
                out=c_qr[bank_no][:].rearrange("p a e c -> p (a e c)"),
                lhsT=cq_words[:, P * r : P * r + P].bitcast(FP8X4), lhsT_scale=cq_scales[:, P * r : P * r + P],
                rhs=wqr_words[:, cols].bitcast(FP8X4), rhs_scale=wqr_scales[:, cols],
                start=True, stop=True,
            )

        def rotate(bank_no):
            r = bank_no % T_TILES
            cr_bank = c_qr[bank_no]
            q_r[bank_no] = results.tile([P, BANK], F32, name="q_r", bufs=3)
            same = results.tile([P, 2, P, 2], F32)
            nc.vector.tensor_tensor(
                out=same[:], in0=cr_bank[:].rearrange("p a e c -> p a c e"),
                in1=cos_pairs[:, r].unsqueeze(1).to_broadcast([P, 2, P, 2]), op=MULT,
            )
            cross = results.tile([P, 2, 2, P], F32)
            nc.vector.tensor_tensor(
                out=cross[:], in0=cr_bank[:, :, ::-1, :],
                in1=sin_signed[:, r].unsqueeze(1).to_broadcast([P, 2, 2, P]), op=MULT,
            )
            nc.gpsimd.tensor_tensor(
                out=q_r[bank_no][:].rearrange("p (a c e) -> p a c e", a=2, e=2),
                in0=same[:], in1=cross[:].rearrange("p a e c -> p a c e"), op=ADD,
            )

        def store_q_r(bank_no):
            b, r = divmod(bank_no, T_TILES)
            nc.sync.dma_start(out=q_r_rows[:, r, BANK * b : BANK * b + BANK], in_=q_r[bank_no][:])

        for j in range(PACK):
            quantise_rows(wdq_raw[:, j, :], wdq_words[:, j, :], wdq_scales[:, j, :])
        for r in range(T_TILES + 2):
            if r < T_TILES:
                quantise_rows(x_raw[:, r, :], x_words[:, r, :], x_scales[:, r, :])
            if r == T_TILES - 1:
                transpose_a(0, BANKS)
            if r >= 2:
                make_c_q(r - 2)
        for i in range(4):
            make_k_eff(0, i, False)
            if i < 2:
                transpose_wqr(0, i, BANKS)
            elif i == 2:
                transpose_a(2, BANKS)
        quantise_wqr(0)
        quantise_k_eff(0)
        for i in range(4):
            make_k_eff(1, i, True)
        make_c_qr(0)

        for h in range(NH):
            next_block = h // T_TILES + 1
            if h % 2 == 1 and h + 3 < NH:
                transpose_a(h + 3, BANKS)
            if h % T_TILES == 0 and next_block < O_BLOCKS:
                transpose_wqr(next_block, 0, BANKS)
            if h % T_TILES == 2 and next_block < O_BLOCKS:
                transpose_wqr(next_block, 1, BANKS)
            rotate(h)
            if h + 1 < NH:
                quantise_k_eff(h + 1)
            if h % T_TILES == 3 and next_block < O_BLOCKS:
                quantise_wqr(next_block)
            for i in range(4):
                make_q_abs(h, i, h < NH - 1 or i % 2 == 1)
                if i == 3 and h + 1 < NH:
                    make_c_qr(h + 1)
                if h + 2 < NH:
                    make_k_eff(h + 2, i, i == 3 or (i == 0 and h % T_TILES == 3))
            store_q_r(h)
